import numpy as np
import ml_dtypes


def mxq(x, axis, fmt="e4m3"):
    dtype, down = {"e4m3": (ml_dtypes.float8_e4m3fn, 7), "e5m2": (ml_dtypes.float8_e5m2, 14)}[fmt]
    v = np.moveaxis(np.asarray(x, np.float32).astype(ml_dtypes.bfloat16).astype(np.float64), axis, -1)
    blocks = v.reshape(v.shape[:-1] + (-1, 32))
    amax = np.abs(blocks).max(-1, keepdims=True)
    byte = np.maximum(np.where(amax > 0, np.frexp(amax)[1] - 1 + 127, 0) - down, 1)
    scale = np.exp2(byte - 127.0)
    codes = (blocks / scale).astype(np.float32).astype(dtype).astype(np.float64)
    return np.moveaxis((codes * scale).reshape(v.shape), -1, axis)


WIDE = False


def mx_kscale(k):
    if not WIDE:
        return np.ones(k)
    levels = np.array([10, -10, 5, -5, 0])
    a = np.random.permutation(np.resize(levels, k // 512 * 4)).reshape(k // 512, 4)
    idx = np.arange(k)
    return np.exp2(a[idx // 512, idx % 128 // 32])


BF16 = ml_dtypes.bfloat16


def bf(x):
    return np.asarray(x, np.float32).astype(BF16)


def f64(x):
    return np.asarray(x).astype(np.float64)


B, C, TC, H, W = 16, 128, 1024, 32, 16
N = H * W
EPS = 1e-6


def setup_inputs():
    s = mx_kscale(TC)
    return {"token": bf(np.random.standard_normal((B, TC, H, W)) * s[None, :, None, None]),
            "Wk": bf(np.random.standard_normal((C, TC)) / np.sqrt(TC) / s[None, :]),
            "Wv": bf(np.random.standard_normal((C, TC)) * 3.0 / np.sqrt(TC) / s[None, :])}


def reference(token, Wk, Wv):
    tq = mxq(f64(token).reshape(B, TC, N), 1, "e4m3")
    kf = mxq(f64(Wk), 1, "e4m3") @ tq
    v = mxq(f64(Wv), 1, "e4m3") @ tq
    vf = v.transpose(0, 2, 1)
    kn = kf / np.maximum(np.sqrt((kf * kf).sum(1, keepdims=True)), EPS)
    return kn, vf

@@ -1,0 +1,188 @@
+from contextlib import ExitStack
+
+import concourse.mybir as mybir
+from concourse.masks import make_identity
+
+BF16 = mybir.dt.bfloat16
+F32 = mybir.dt.float32
+U32 = mybir.dt.uint32
+U8 = mybir.dt.uint8
+FP8X4 = mybir.dt.float8_e4m3fn_x4
+ACT = mybir.ActivationFunctionType
+ALU = mybir.AluOpType
+
+P = 128
+PACK = 4
+K_PASS = P * PACK
+IMAGES = 16
+CHANNELS_IN = 1024
+CHANNELS_OUT = 128
+PIXELS = 512
+PASSES = CHANNELS_IN // K_PASS
+SLICES = PIXELS // P
+EPS = 1e-6
+RUN = 4
+VECTOR_PIXELS = 160
+LOADS_AHEAD = 6
+
+FLOPS = 2 * 2 * IMAGES * CHANNELS_OUT * CHANNELS_IN * PIXELS
+
+
+def tile_trgramkqv_pa_t_kernel(tc, token, Wk, Wv, out_0, out_1):
+    nc = tc.nc
+    with ExitStack() as ctx:
+        const = ctx.enter_context(tc.tile_pool(name="const", bufs=1))
+        raw_pool = ctx.enter_context(tc.tile_pool(name="raw", bufs=LOADS_AHEAD + 2))
+        stage = ctx.enter_context(tc.tile_pool(name="stage", bufs=3))
+        result = ctx.enter_context(tc.tile_pool(name="result", bufs=3))
+        psum = ctx.enter_context(tc.psum_pool(name="psum", bufs=2))
+        ctx.enter_context(tc.manual_schedule())
+
+        raw = {}
+        grouped = {}
+        codes = {}
+        scales = {}
+        k_acc = {}
+        v_acc = {}
+        sums = {}
+        inverse = {}
+
+        def load(b, passes):
+            if b not in raw:
+                raw[b] = raw_pool.tile([P, PASSES, PACK, PIXELS], BF16, name="raw")
+            nc.sync.dma_start(
+                out=raw[b][:, passes].rearrange("p g t n -> p g (t n)"),
+                in_=token[b].rearrange("(g p t) h w -> p g (t h w)", g=PASSES, p=P, t=PACK)[
+                    :, passes
+                ],
+            )
+
+        def regroup(b):
+            grouped[b] = stage.tile([P, PASSES, PIXELS, PACK], BF16, align_bytes=64, name="grouped")
+            for copy, g, pixels in (
+                (nc.vector.tensor_copy, 0, slice(0, PIXELS)),
+                (nc.vector.tensor_copy, 1, slice(0, VECTOR_PIXELS)),
+                (nc.scalar.copy, 1, slice(VECTOR_PIXELS, PIXELS)),
+            ):
+                copy(
+                    out=grouped[b][:, g, pixels, :].rearrange("p (c i) t -> p c t i", i=RUN),
+                    in_=raw[b][:, g, :, pixels].rearrange("p t (c i) -> p c t i", i=RUN),
+                )
+
+        def quantise(b):
+            codes[b] = stage.tile([P, PASSES, PIXELS], U32, align_bytes=64, name="codes")
+            scales[b] = stage.tile([P, PASSES, PIXELS], U8, align_bytes=64, name="scales")
+            nc.vector.quantize_mx(
+                out=codes[b][:].rearrange("p g n -> p (g n)").bitcast(FP8X4),
+                scales=scales[b][:].rearrange("p g n -> p (g n)"),
+                in_=grouped[b][:].rearrange("p g n t -> p (g n t)"),
+            )
+
+        def multiply(b):
+            k_acc[b] = psum.tile([P, PIXELS], F32, name="k_acc", bufs=3)
+            for g in range(PASSES):
+                nc.tensor.matmul_mx(
+                    out=k_acc[b][:],
+                    lhsT=w_codes[:, g, 0, :].bitcast(FP8X4),
+                    lhsT_scale=w_scales[:, g, 0, :],
+                    rhs=codes[b][:, g, :].bitcast(FP8X4),
+                    rhs_scale=scales[b][:, g, :],
+                    start=(g == 0),
+                    stop=(g == PASSES - 1),
+                )
+            v_acc[b] = psum.tile([P, SLICES, CHANNELS_OUT], F32, name="v_acc")
+            for s in range(SLICES):
+                pixels = slice(s * P, (s + 1) * P)
+                for g in range(PASSES):
+                    nc.tensor.matmul_mx(
+                        out=v_acc[b][:, s, :],
+                        lhsT=codes[b][:, g, pixels].bitcast(FP8X4),
+                        lhsT_scale=scales[b][:, g, pixels],
+                        rhs=w_codes[:, g, 1, :].bitcast(FP8X4),
+                        rhs_scale=w_scales[:, g, 1, :],
+                        start=(g == 0),
+                        stop=(g == PASSES - 1),
+                    )
+
+        def sum_squares(b):
+            squares = result.tile([P, PIXELS], F32, name="squares")
+            nc.scalar.activation(out=squares[:], in_=k_acc[b][:], func=ACT.Square)
+            sums[b] = psum.tile([P, PIXELS], F32, name="sums")
+            nc.tensor.matmul(out=sums[b][:], lhsT=ones[:], rhs=squares[:], start=True, stop=True)
+
+        def store_v(b):
+            vf = result.tile([P, SLICES, CHANNELS_OUT], F32, name="vf")
+            nc.scalar.copy(out=vf[:], in_=v_acc[b][:])
+            nc.sync.dma_start(out=out_1[b].rearrange("(s p) c -> p s c", p=P), in_=vf[:])
+
+        def invert_norm(b):
+            inverse[b] = result.tile([P, PIXELS], F32, name="inverse")
+            nc.scalar.activation(out=inverse[b][:], in_=sums[b][:], func=ACT.Abs_reciprocal_sqrt)
+
+        def store_k(b):
+            kn = result.tile([P, PIXELS], F32, name="kn")
+            nc.vector.scalar_tensor_tensor(
+                out=kn[:],
+                in0=inverse[b][:],
+                scalar=1.0 / EPS,
+                in1=k_acc[b][:],
+                op0=ALU.min,
+                op1=ALU.mult,
+            )
+            nc.sync.dma_start(out=out_0[b], in_=kn[:])
+
+        w_raw = const.tile([P, 2, CHANNELS_IN], BF16)
+        load(0, slice(0, 1))
+        load(0, slice(1, PASSES))
+        nc.sync.dma_start(out=w_raw[:, 0, :], in_=Wk)
+        nc.sync.dma_start(out=w_raw[:, 1, :], in_=Wv)
+        for b in range(1, LOADS_AHEAD):
+            load(b, slice(0, PASSES))
+
+        ident = const.tile([P, P], F32)
+        make_identity(nc, ident[:])
+        ones = const.tile([P, P], F32)
+        nc.vector.memset(ones[:], 1.0)
+        warm = const.tile([P, 1], F32)
+        nc.scalar.activation(out=warm[:], in_=ones[:, 0:1], func=ACT.Abs_reciprocal_sqrt)
+
+        regroup(0)
+        quantise(0)
+
+        w_words = w_raw[:].bitcast(F32).rearrange("c w (g p u) -> c w g u p", g=PASSES, p=P, u=2)
+        w_grouped = const.tile([P, PASSES * 2 * CHANNELS_OUT * PACK], BF16, align_bytes=64)
+        w_grouped_words = w_grouped[:].bitcast(F32).rearrange(
+            "p (g w c u) -> p g w c u", g=PASSES, w=2, c=CHANNELS_OUT, u=2
+        )
+        w_codes = const.tile([P, PASSES, 2, CHANNELS_OUT], U32, align_bytes=64)
+        w_scales = const.tile([P, PASSES, 2, CHANNELS_OUT], U8, align_bytes=64)
+        wt = {}
+        for g in range(PASSES):
+            wt[g] = psum.tile([P, 2, 2, CHANNELS_OUT], F32, name="wt", tag="sums")
+            for w in range(2):
+                for u in range(2):
+                    nc.tensor.transpose(wt[g][:, w, u, :], w_words[:, w, g, u, :], ident[:])
+        for g, copy in ((0, nc.vector.tensor_copy), (1, nc.scalar.copy)):
+            copy(out=w_grouped_words[:, g], in_=wt[g][:].rearrange("p w u c -> p w c u"))
+        nc.vector.quantize_mx(
+            out=w_codes[:].rearrange("p g w c -> p (g w c)").bitcast(FP8X4),
+            scales=w_scales[:].rearrange("p g w c -> p (g w c)"),
+            in_=w_grouped[:],
+        )
+
+        for b in range(IMAGES + 2):
+            if b < IMAGES:
+                multiply(b)
+            if b + 1 < IMAGES:
+                regroup(b + 1)
+            if 0 <= b - 1 < IMAGES:
+                invert_norm(b - 1)
+            if b < IMAGES:
+                sum_squares(b)
+                store_v(b)
+            if 0 <= b - 2:
+                store_k(b - 2)
+            if b + 1 < IMAGES:
+                quantise(b + 1)
+            if b + LOADS_AHEAD < IMAGES:
+                load(b + LOADS_AHEAD, slice(0, PASSES))

@@ -23,7 +23,7 @@ SLICES = PIXELS // P
 EPS = 1e-6
 RUN = 4
 VECTOR_PIXELS = 160
-LOADS_AHEAD = 6
+STORES_WAITING = 10
 
 FLOPS = 2 * 2 * IMAGES * CHANNELS_OUT * CHANNELS_IN * PIXELS
 
@@ -32,9 +32,10 @@ def tile_trgramkqv_pa_t_kernel(tc, token, Wk, Wv, out_0, out_1):
     nc = tc.nc
     with ExitStack() as ctx:
         const = ctx.enter_context(tc.tile_pool(name="const", bufs=1))
-        raw_pool = ctx.enter_context(tc.tile_pool(name="raw", bufs=LOADS_AHEAD + 2))
+        raw_pool = ctx.enter_context(tc.tile_pool(name="raw", bufs=IMAGES))
         stage = ctx.enter_context(tc.tile_pool(name="stage", bufs=3))
-        result = ctx.enter_context(tc.tile_pool(name="result", bufs=3))
+        norm = ctx.enter_context(tc.tile_pool(name="norm", bufs=3))
+        result = ctx.enter_context(tc.tile_pool(name="result", bufs=STORES_WAITING))
         psum = ctx.enter_context(tc.psum_pool(name="psum", bufs=2))
         ctx.enter_context(tc.manual_schedule())
 
@@ -58,7 +59,7 @@ def tile_trgramkqv_pa_t_kernel(tc, token, Wk, Wv, out_0, out_1):
             )
 
         def regroup(b):
-            grouped[b] = stage.tile([P, PASSES, PIXELS, PACK], BF16, align_bytes=64, name="grouped")
+            grouped[b] = stage.tile([P, PASSES, PIXELS, PACK], BF16, align_bytes=64, name="grouped", bufs=2)
             for copy, g, pixels in (
                 (nc.vector.tensor_copy, 0, slice(0, PIXELS)),
                 (nc.vector.tensor_copy, 1, slice(0, VECTOR_PIXELS)),
@@ -105,7 +106,7 @@ def tile_trgramkqv_pa_t_kernel(tc, token, Wk, Wv, out_0, out_1):
                     )
 
         def sum_squares(b):
-            squares = result.tile([P, PIXELS], F32, name="squares")
+            squares = norm.tile([P, PIXELS], F32, name="squares")
             nc.scalar.activation(out=squares[:], in_=k_acc[b][:], func=ACT.Square)
             sums[b] = psum.tile([P, PIXELS], F32, name="sums")
             nc.tensor.matmul(out=sums[b][:], lhsT=ones[:], rhs=squares[:], start=True, stop=True)
@@ -116,7 +117,7 @@ def tile_trgramkqv_pa_t_kernel(tc, token, Wk, Wv, out_0, out_1):
             nc.sync.dma_start(out=out_1[b].rearrange("(s p) c -> p s c", p=P), in_=vf[:])
 
         def invert_norm(b):
-            inverse[b] = result.tile([P, PIXELS], F32, name="inverse")
+            inverse[b] = norm.tile([P, PIXELS], F32, name="inverse")
             nc.scalar.activation(out=inverse[b][:], in_=sums[b][:], func=ACT.Abs_reciprocal_sqrt)
 
         def store_k(b):
@@ -136,7 +137,7 @@ def tile_trgramkqv_pa_t_kernel(tc, token, Wk, Wv, out_0, out_1):
         load(0, slice(1, PASSES))
         nc.sync.dma_start(out=w_raw[:, 0, :], in_=Wk)
         nc.sync.dma_start(out=w_raw[:, 1, :], in_=Wv)
-        for b in range(1, LOADS_AHEAD):
+        for b in range(1, IMAGES):
             load(b, slice(0, PASSES))
 
         ident = const.tile([P, P], F32)
@@ -184,5 +185,3 @@ def tile_trgramkqv_pa_t_kernel(tc, token, Wk, Wv, out_0, out_1):
                 store_k(b - 2)
             if b + 1 < IMAGES:
                 quantise(b + 1)
-            if b + LOADS_AHEAD < IMAGES:
-                load(b + LOADS_AHEAD, slice(0, PASSES))

@@ -22,7 +22,8 @@ PASSES = CHANNELS_IN // K_PASS
 SLICES = PIXELS // P
 EPS = 1e-6
 RUN = 4
-VECTOR_PIXELS = 160
+VECTOR_PIXELS = 312
+SCALAR_PIXELS = 168
 STORES_WAITING = 10
 
 FLOPS = 2 * 2 * IMAGES * CHANNELS_OUT * CHANNELS_IN * PIXELS
@@ -58,16 +59,26 @@ def tile_trgramkqv_pa_t_kernel(tc, token, Wk, Wv, out_0, out_1):
                 ],
             )
 
-        def regroup(b):
-            grouped[b] = stage.tile([P, PASSES, PIXELS, PACK], BF16, align_bytes=64, name="grouped", bufs=2)
-            for copy, g, pixels in (
-                (nc.vector.tensor_copy, 0, slice(0, PIXELS)),
-                (nc.vector.tensor_copy, 1, slice(0, VECTOR_PIXELS)),
-                (nc.scalar.copy, 1, slice(VECTOR_PIXELS, PIXELS)),
-            ):
-                copy(
-                    out=grouped[b][:, g, pixels, :].rearrange("p (c i) t -> p c t i", i=RUN),
-                    in_=raw[b][:, g, :, pixels].rearrange("p t (c i) -> p c t i", i=RUN),
+        def regroup(b, pass_groups):
+            if b not in grouped:
+                grouped[b] = stage.tile([P, PASSES, PIXELS, PACK], BF16, align_bytes=64, name="grouped", bufs=2)
+            for passes in pass_groups:
+                for copy, pixels in (
+                    (nc.vector.tensor_copy, slice(0, VECTOR_PIXELS)),
+                    (nc.scalar.copy, slice(VECTOR_PIXELS, VECTOR_PIXELS + SCALAR_PIXELS)),
+                ):
+                    copy(
+                        out=grouped[b][:, passes, pixels, :].rearrange("p g (c i) t -> p g c t i", i=RUN),
+                        in_=raw[b][:, passes, :, pixels].rearrange("p g t (c i) -> p g c t i", i=RUN),
+                    )
+                pixels = slice(VECTOR_PIXELS + SCALAR_PIXELS, PIXELS)
+                nc.gpsimd.tensor_scalar(
+                    out=grouped[b][:, passes, pixels, :],
+                    in0=raw[b][:, passes, :, pixels].rearrange("p g t n -> p g n t"),
+                    scalar1=1.0,
+                    scalar2=0.0,
+                    op0=ALU.mult,
+                    op1=ALU.add,
                 )
 
         def quantise(b):
@@ -147,7 +158,7 @@ def tile_trgramkqv_pa_t_kernel(tc, token, Wk, Wv, out_0, out_1):
         warm = const.tile([P, 1], F32)
         nc.scalar.activation(out=warm[:], in_=ones[:, 0:1], func=ACT.Abs_reciprocal_sqrt)
 
-        regroup(0)
+        regroup(0, (slice(0, 1), slice(1, PASSES)))
         quantise(0)
 
         w_words = w_raw[:].bitcast(F32).rearrange("c w (g p u) -> c w g u p", g=PASSES, p=P, u=2)
@@ -170,18 +181,21 @@ def tile_trgramkqv_pa_t_kernel(tc, token, Wk, Wv, out_0, out_1):
             scales=w_scales[:].rearrange("p g w c -> p (g w c)"),
             in_=w_grouped[:],
         )
+        regroup(1, (slice(0, PASSES),))
 
         for b in range(IMAGES + 2):
+            if 2 <= b < IMAGES:
+                quantise(b)
             if b < IMAGES:
                 multiply(b)
-            if b + 1 < IMAGES:
-                regroup(b + 1)
-            if 0 <= b - 1 < IMAGES:
-                invert_norm(b - 1)
+            if 0 <= b - 2:
+                store_k(b - 2)
             if b < IMAGES:
                 sum_squares(b)
                 store_v(b)
-            if 0 <= b - 2:
-                store_k(b - 2)
-            if b + 1 < IMAGES:
-                quantise(b + 1)
+            if b == 0:
+                quantise(1)
+            if b + 2 < IMAGES:
+                regroup(b + 2, (slice(0, PASSES),))
+            if b < IMAGES:
+                invert_norm(b)

@@ -24,6 +24,7 @@ EPS = 1e-6
 RUN = 4
 VECTOR_PIXELS = 312
 SCALAR_PIXELS = 168
+LAST_SHIFT = 32
 STORES_WAITING = 10
 
 FLOPS = 2 * 2 * IMAGES * CHANNELS_OUT * CHANNELS_IN * PIXELS
@@ -46,6 +47,7 @@ def tile_trgramkqv_pa_t_kernel(tc, token, Wk, Wv, out_0, out_1):
         scales = {}
         k_acc = {}
         v_acc = {}
+        squares = {}
         sums = {}
         inverse = {}
 
@@ -60,18 +62,20 @@ def tile_trgramkqv_pa_t_kernel(tc, token, Wk, Wv, out_0, out_1):
             )
 
         def regroup(b, pass_groups):
+            vector_pixels = VECTOR_PIXELS + (LAST_SHIFT if b == IMAGES - 1 else 0)
+            gpsimd_from = VECTOR_PIXELS + SCALAR_PIXELS
             if b not in grouped:
                 grouped[b] = stage.tile([P, PASSES, PIXELS, PACK], BF16, align_bytes=64, name="grouped", bufs=2)
             for passes in pass_groups:
                 for copy, pixels in (
-                    (nc.vector.tensor_copy, slice(0, VECTOR_PIXELS)),
-                    (nc.scalar.copy, slice(VECTOR_PIXELS, VECTOR_PIXELS + SCALAR_PIXELS)),
+                    (nc.vector.tensor_copy, slice(0, vector_pixels)),
+                    (nc.scalar.copy, slice(vector_pixels, gpsimd_from)),
                 ):
                     copy(
                         out=grouped[b][:, passes, pixels, :].rearrange("p g (c i) t -> p g c t i", i=RUN),
                         in_=raw[b][:, passes, :, pixels].rearrange("p g t (c i) -> p g c t i", i=RUN),
                     )
-                pixels = slice(VECTOR_PIXELS + SCALAR_PIXELS, PIXELS)
+                pixels = slice(gpsimd_from, PIXELS)
                 nc.gpsimd.tensor_scalar(
                     out=grouped[b][:, passes, pixels, :],
                     in0=raw[b][:, passes, :, pixels].rearrange("p g t n -> p g n t"),
@@ -90,8 +94,8 @@ def tile_trgramkqv_pa_t_kernel(tc, token, Wk, Wv, out_0, out_1):
                 in_=grouped[b][:].rearrange("p g n t -> p (g n t)"),
             )
 
-        def multiply(b):
-            k_acc[b] = psum.tile([P, PIXELS], F32, name="k_acc", bufs=3)
+        def multiply_k(b):
+            k_acc[b] = psum.tile([P, PIXELS], F32, name="k_acc", bufs=4)
             for g in range(PASSES):
                 nc.tensor.matmul_mx(
                     out=k_acc[b][:],
@@ -102,6 +106,8 @@ def tile_trgramkqv_pa_t_kernel(tc, token, Wk, Wv, out_0, out_1):
                     start=(g == 0),
                     stop=(g == PASSES - 1),
                 )
+
+        def multiply_v(b):
             v_acc[b] = psum.tile([P, SLICES, CHANNELS_OUT], F32, name="v_acc")
             for s in range(SLICES):
                 pixels = slice(s * P, (s + 1) * P)
@@ -116,11 +122,13 @@ def tile_trgramkqv_pa_t_kernel(tc, token, Wk, Wv, out_0, out_1):
                         stop=(g == PASSES - 1),
                     )
 
+        def square(b):
+            squares[b] = norm.tile([P, PIXELS], F32, name="squares")
+            nc.scalar.activation(out=squares[b][:], in_=k_acc[b][:], func=ACT.Square)
+
         def sum_squares(b):
-            squares = norm.tile([P, PIXELS], F32, name="squares")
-            nc.scalar.activation(out=squares[:], in_=k_acc[b][:], func=ACT.Square)
             sums[b] = psum.tile([P, PIXELS], F32, name="sums")
-            nc.tensor.matmul(out=sums[b][:], lhsT=ones[:], rhs=squares[:], start=True, stop=True)
+            nc.tensor.matmul(out=sums[b][:], lhsT=ones[:], rhs=squares[b][:], start=True, stop=True)
 
         def store_v(b):
             vf = result.tile([P, SLICES, CHANNELS_OUT], F32, name="vf")
@@ -183,19 +191,37 @@ def tile_trgramkqv_pa_t_kernel(tc, token, Wk, Wv, out_0, out_1):
         )
         regroup(1, (slice(0, PASSES),))
 
-        for b in range(IMAGES + 2):
-            if 2 <= b < IMAGES:
+        for b in range(IMAGES - 2):
+            if 2 <= b:
                 quantise(b)
-            if b < IMAGES:
-                multiply(b)
+            multiply_k(b)
+            multiply_v(b)
             if 0 <= b - 2:
                 store_k(b - 2)
-            if b < IMAGES:
-                sum_squares(b)
-                store_v(b)
+            square(b)
+            sum_squares(b)
+            store_v(b)
             if b == 0:
                 quantise(1)
-            if b + 2 < IMAGES:
-                regroup(b + 2, (slice(0, PASSES),))
-            if b < IMAGES:
-                invert_norm(b)
+            regroup(b + 2, (slice(0, PASSES),))
+            invert_norm(b)
+
+        last = IMAGES - 1
+        quantise(last - 1)
+        multiply_k(last - 1)
+        multiply_v(last - 1)
+        quantise(last)
+        square(last - 1)
+        multiply_k(last)
+        sum_squares(last - 1)
+        store_v(last - 1)
+        store_k(last - 3)
+        square(last)
+        sum_squares(last)
+        invert_norm(last - 1)
+        multiply_v(last)
+        store_k(last - 2)
+        invert_norm(last)
+        store_k(last - 1)
+        store_v(last)
+        store_k(last)

@@ -21,7 +21,7 @@ PIXELS = 512
 PASSES = CHANNELS_IN // K_PASS
 SLICES = PIXELS // P
 EPS = 1e-6
-RUN = 4
+RUN = 8
 VECTOR_PIXELS = 312
 SCALAR_PIXELS = 168
 LAST_SHIFT = 32

@@ -27,6 +27,9 @@ SCALAR_PIXELS = 168
 LAST_SHIFT = 32
 STORES_WAITING = 10
 
+WHOLE = range(SLICES)
+HALVES = (range(0, SLICES // 2), range(SLICES // 2, SLICES))
+
 FLOPS = 2 * 2 * IMAGES * CHANNELS_OUT * CHANNELS_IN * PIXELS
 
 
@@ -107,13 +110,13 @@ def tile_trgramkqv_pa_t_kernel(tc, token, Wk, Wv, out_0, out_1):
                     stop=(g == PASSES - 1),
                 )
 
-        def multiply_v(b):
-            v_acc[b] = psum.tile([P, SLICES, CHANNELS_OUT], F32, name="v_acc")
-            for s in range(SLICES):
+        def multiply_v(b, part=WHOLE):
+            v_acc[b, part] = psum.tile([P, len(part), CHANNELS_OUT], F32, name="v_acc")
+            for s in part:
                 pixels = slice(s * P, (s + 1) * P)
                 for g in range(PASSES):
                     nc.tensor.matmul_mx(
-                        out=v_acc[b][:, s, :],
+                        out=v_acc[b, part][:, s - part.start, :],
                         lhsT=codes[b][:, g, pixels].bitcast(FP8X4),
                         lhsT_scale=scales[b][:, g, pixels],
                         rhs=w_codes[:, g, 1, :].bitcast(FP8X4),
@@ -126,30 +129,37 @@ def tile_trgramkqv_pa_t_kernel(tc, token, Wk, Wv, out_0, out_1):
             squares[b] = norm.tile([P, PIXELS], F32, name="squares")
             nc.scalar.activation(out=squares[b][:], in_=k_acc[b][:], func=ACT.Square)
 
-        def sum_squares(b):
-            sums[b] = psum.tile([P, PIXELS], F32, name="sums")
-            nc.tensor.matmul(out=sums[b][:], lhsT=ones[:], rhs=squares[b][:], start=True, stop=True)
+        def pixels_of(part):
+            return slice(part.start * P, part.stop * P)
 
-        def store_v(b):
-            vf = result.tile([P, SLICES, CHANNELS_OUT], F32, name="vf")
-            nc.scalar.copy(out=vf[:], in_=v_acc[b][:])
-            nc.sync.dma_start(out=out_1[b].rearrange("(s p) c -> p s c", p=P), in_=vf[:])
+        def sum_squares(b, part=WHOLE):
+            sums[b, part] = psum.tile([P, len(part) * P], F32, name="sums")
+            nc.tensor.matmul(
+                out=sums[b, part][:], lhsT=ones[:], rhs=squares[b][:, pixels_of(part)], start=True, stop=True
+            )
 
-        def invert_norm(b):
-            inverse[b] = norm.tile([P, PIXELS], F32, name="inverse")
-            nc.scalar.activation(out=inverse[b][:], in_=sums[b][:], func=ACT.Abs_reciprocal_sqrt)
+        def store_v(b, part=WHOLE):
+            vf = result.tile([P, len(part), CHANNELS_OUT], F32, name="vf")
+            nc.scalar.copy(out=vf[:], in_=v_acc[b, part][:])
+            nc.sync.dma_start(
+                out=out_1[b].rearrange("(s p) c -> p s c", p=P)[:, part.start : part.stop, :], in_=vf[:]
+            )
 
-        def store_k(b):
-            kn = result.tile([P, PIXELS], F32, name="kn")
+        def invert_norm(b, part=WHOLE):
+            inverse[b, part] = norm.tile([P, len(part) * P], F32, name="inverse")
+            nc.scalar.activation(out=inverse[b, part][:], in_=sums[b, part][:], func=ACT.Abs_reciprocal_sqrt)
+
+        def store_k(b, part=WHOLE):
+            kn = result.tile([P, len(part) * P], F32, name="kn")
             nc.vector.scalar_tensor_tensor(
                 out=kn[:],
-                in0=inverse[b][:],
+                in0=inverse[b, part][:],
                 scalar=1.0 / EPS,
-                in1=k_acc[b][:],
+                in1=k_acc[b][:, pixels_of(part)],
                 op0=ALU.min,
                 op1=ALU.mult,
             )
-            nc.sync.dma_start(out=out_0[b], in_=kn[:])
+            nc.sync.dma_start(out=out_0[b][:, pixels_of(part)], in_=kn[:])
 
         w_raw = const.tile([P, 2, CHANNELS_IN], BF16)
         load(0, slice(0, 1))
@@ -217,11 +227,15 @@ def tile_trgramkqv_pa_t_kernel(tc, token, Wk, Wv, out_0, out_1):
         store_v(last - 1)
         store_k(last - 3)
         square(last)
-        sum_squares(last)
         invert_norm(last - 1)
-        multiply_v(last)
+        for half in HALVES:
+            sum_squares(last, half)
+        for half in HALVES:
+            multiply_v(last, half)
         store_k(last - 2)
-        invert_norm(last)
         store_k(last - 1)
-        store_v(last)
-        store_k(last)
+        for half in HALVES:
+            invert_norm(last, half)
+        for half in HALVES:
+            store_k(last, half)
+            store_v(last, half)

@@ -22,9 +22,9 @@ PASSES = CHANNELS_IN // K_PASS
 SLICES = PIXELS // P
 EPS = 1e-6
 RUN = 8
-VECTOR_PIXELS = 312
+VECTOR_PIXELS = 304
 SCALAR_PIXELS = 168
-LAST_SHIFT = 32
+LAST_SHIFT = 40
 STORES_WAITING = 10
 
 WHOLE = range(SLICES)

@@ -25,7 +25,7 @@ RUN = 8
 VECTOR_PIXELS = 304
 SCALAR_PIXELS = 168
 LAST_SHIFT = 40
-STORES_WAITING = 10
+STORES_WAITING = 13
 
 WHOLE = range(SLICES)
 HALVES = (range(0, SLICES // 2), range(SLICES // 2, SLICES))

@@ -25,7 +25,9 @@ RUN = 8
 VECTOR_PIXELS = 304
 SCALAR_PIXELS = 168
 LAST_SHIFT = 40
-STORES_WAITING = 13
+FIRST_IMAGES = 3
+FIRST_VECTOR_PIXELS = 328
+STORES_WAITING = 10
 
 WHOLE = range(SLICES)
 HALVES = (range(0, SLICES // 2), range(SLICES // 2, SLICES))
@@ -65,8 +67,11 @@ def tile_trgramkqv_pa_t_kernel(tc, token, Wk, Wv, out_0, out_1):
             )
 
         def regroup(b, pass_groups):
-            vector_pixels = VECTOR_PIXELS + (LAST_SHIFT if b == IMAGES - 1 else 0)
-            gpsimd_from = VECTOR_PIXELS + SCALAR_PIXELS
+            if b < FIRST_IMAGES:
+                vector_pixels, gpsimd_from = FIRST_VECTOR_PIXELS, PIXELS
+            else:
+                vector_pixels = VECTOR_PIXELS + (LAST_SHIFT if b == IMAGES - 1 else 0)
+                gpsimd_from = VECTOR_PIXELS + SCALAR_PIXELS
             if b not in grouped:
                 grouped[b] = stage.tile([P, PASSES, PIXELS, PACK], BF16, align_bytes=64, name="grouped", bufs=2)
             for passes in pass_groups:
@@ -78,15 +83,16 @@ def tile_trgramkqv_pa_t_kernel(tc, token, Wk, Wv, out_0, out_1):
                         out=grouped[b][:, passes, pixels, :].rearrange("p g (c i) t -> p g c t i", i=RUN),
                         in_=raw[b][:, passes, :, pixels].rearrange("p g t (c i) -> p g c t i", i=RUN),
                     )
-                pixels = slice(gpsimd_from, PIXELS)
-                nc.gpsimd.tensor_scalar(
-                    out=grouped[b][:, passes, pixels, :],
-                    in0=raw[b][:, passes, :, pixels].rearrange("p g t n -> p g n t"),
-                    scalar1=1.0,
-                    scalar2=0.0,
-                    op0=ALU.mult,
-                    op1=ALU.add,
-                )
+                if gpsimd_from < PIXELS:
+                    pixels = slice(gpsimd_from, PIXELS)
+                    nc.gpsimd.tensor_scalar(
+                        out=grouped[b][:, passes, pixels, :],
+                        in0=raw[b][:, passes, :, pixels].rearrange("p g t n -> p g n t"),
+                        scalar1=1.0,
+                        scalar2=0.0,
+                        op0=ALU.mult,
+                        op1=ALU.add,
+                    )
 
         def quantise(b):
             codes[b] = stage.tile([P, PASSES, PIXELS], U32, align_bytes=64, name="codes")

@@ -26,7 +26,7 @@ VECTOR_PIXELS = 304
 SCALAR_PIXELS = 168
 LAST_SHIFT = 40
 FIRST_IMAGES = 3
-FIRST_VECTOR_PIXELS = 328
+FIRST_VECTOR_PIXELS = 312
 STORES_WAITING = 10
 
 WHOLE = range(SLICES)
@@ -108,8 +108,8 @@ def tile_trgramkqv_pa_t_kernel(tc, token, Wk, Wv, out_0, out_1):
             for g in range(PASSES):
                 nc.tensor.matmul_mx(
                     out=k_acc[b][:],
-                    lhsT=w_codes[:, g, 0, :].bitcast(FP8X4),
-                    lhsT_scale=w_scales[:, g, 0, :],
+                    lhsT=w_codes[:, 0, g, :].bitcast(FP8X4),
+                    lhsT_scale=w_scales[:, 0, g, :],
                     rhs=codes[b][:, g, :].bitcast(FP8X4),
                     rhs_scale=scales[b][:, g, :],
                     start=(g == 0),
@@ -125,8 +125,8 @@ def tile_trgramkqv_pa_t_kernel(tc, token, Wk, Wv, out_0, out_1):
                         out=v_acc[b, part][:, s - part.start, :],
                         lhsT=codes[b][:, g, pixels].bitcast(FP8X4),
                         lhsT_scale=scales[b][:, g, pixels],
-                        rhs=w_codes[:, g, 1, :].bitcast(FP8X4),
-                        rhs_scale=w_scales[:, g, 1, :],
+                        rhs=w_codes[:, 1, g, :].bitcast(FP8X4),
+                        rhs_scale=w_scales[:, 1, g, :],
                         start=(g == 0),
                         stop=(g == PASSES - 1),
                     )
@@ -139,7 +139,8 @@ def tile_trgramkqv_pa_t_kernel(tc, token, Wk, Wv, out_0, out_1):
             return slice(part.start * P, part.stop * P)
 
         def sum_squares(b, part=WHOLE):
-            sums[b, part] = psum.tile([P, len(part) * P], F32, name="sums")
+            tag, bufs = ("k_acc", 4) if b == IMAGES - 1 else ("sums", 2)
+            sums[b, part] = psum.tile([P, len(part) * P], F32, name="sums", tag=tag, bufs=bufs)
             nc.tensor.matmul(
                 out=sums[b, part][:], lhsT=ones[:], rhs=squares[b][:, pixels_of(part)], start=True, stop=True
             )
@@ -172,7 +173,9 @@ def tile_trgramkqv_pa_t_kernel(tc, token, Wk, Wv, out_0, out_1):
         load(0, slice(1, PASSES))
         nc.sync.dma_start(out=w_raw[:, 0, :], in_=Wk)
         nc.sync.dma_start(out=w_raw[:, 1, :], in_=Wv)
-        for b in range(1, IMAGES):
+        load(1, slice(0, 1))
+        load(1, slice(1, PASSES))
+        for b in range(2, IMAGES):
             load(b, slice(0, PASSES))
 
         ident = const.tile([P, P], F32)
@@ -186,26 +189,24 @@ def tile_trgramkqv_pa_t_kernel(tc, token, Wk, Wv, out_0, out_1):
         quantise(0)
 
         w_words = w_raw[:].bitcast(F32).rearrange("c w (g p u) -> c w g u p", g=PASSES, p=P, u=2)
-        w_grouped = const.tile([P, PASSES * 2 * CHANNELS_OUT * PACK], BF16, align_bytes=64)
-        w_grouped_words = w_grouped[:].bitcast(F32).rearrange(
-            "p (g w c u) -> p g w c u", g=PASSES, w=2, c=CHANNELS_OUT, u=2
-        )
-        w_codes = const.tile([P, PASSES, 2, CHANNELS_OUT], U32, align_bytes=64)
-        w_scales = const.tile([P, PASSES, 2, CHANNELS_OUT], U8, align_bytes=64)
-        wt = {}
-        for g in range(PASSES):
-            wt[g] = psum.tile([P, 2, 2, CHANNELS_OUT], F32, name="wt", tag="sums")
-            for w in range(2):
+        w_grouped = const.tile([P, 2, PASSES * CHANNELS_OUT * PACK], BF16, align_bytes=64)
+        w_codes = const.tile([P, 2, PASSES, CHANNELS_OUT], U32, align_bytes=64)
+        w_scales = const.tile([P, 2, PASSES, CHANNELS_OUT], U8, align_bytes=64)
+        for w in range(2):
+            wt = psum.tile([P, PASSES, 2, CHANNELS_OUT], F32, name="wt", tag="sums")
+            for g in range(PASSES):
                 for u in range(2):
-                    nc.tensor.transpose(wt[g][:, w, u, :], w_words[:, w, g, u, :], ident[:])
-        for g, copy in ((0, nc.vector.tensor_copy), (1, nc.scalar.copy)):
-            copy(out=w_grouped_words[:, g], in_=wt[g][:].rearrange("p w u c -> p w c u"))
-        nc.vector.quantize_mx(
-            out=w_codes[:].rearrange("p g w c -> p (g w c)").bitcast(FP8X4),
-            scales=w_scales[:].rearrange("p g w c -> p (g w c)"),
-            in_=w_grouped[:],
-        )
-        regroup(1, (slice(0, PASSES),))
+                    nc.tensor.transpose(wt[:, g, u, :], w_words[:, w, g, u, :], ident[:])
+            nc.scalar.copy(
+                out=w_grouped[:, w, :].bitcast(F32).rearrange("p (g c u) -> p g c u", g=PASSES, u=2),
+                in_=wt[:].rearrange("p g u c -> p g c u"),
+            )
+            nc.vector.quantize_mx(
+                out=w_codes[:, w].rearrange("p g c -> p (g c)").bitcast(FP8X4),
+                scales=w_scales[:, w].rearrange("p g c -> p (g c)"),
+                in_=w_grouped[:, w, :],
+            )
+        regroup(1, (slice(0, 1), slice(1, PASSES)))
 
         for b in range(IMAGES - 2):
             if 2 <= b:
@@ -229,17 +230,20 @@ def tile_trgramkqv_pa_t_kernel(tc, token, Wk, Wv, out_0, out_1):
         quantise(last)
         square(last - 1)
         multiply_k(last)
-        sum_squares(last - 1)
-        store_v(last - 1)
+        for half in HALVES:
+            sum_squares(last - 1, half)
         store_k(last - 3)
+        store_v(last - 1)
+        store_k(last - 2)
         square(last)
-        invert_norm(last - 1)
+        for half in HALVES:
+            invert_norm(last - 1, half)
         for half in HALVES:
             sum_squares(last, half)
         for half in HALVES:
             multiply_v(last, half)
-        store_k(last - 2)
-        store_k(last - 1)
+        for half in HALVES:
+            store_k(last - 1, half)
         for half in HALVES:
             invert_norm(last, half)
         for half in HALVES:

@@ -21,10 +21,14 @@ PIXELS = 512
 PASSES = CHANNELS_IN // K_PASS
 SLICES = PIXELS // P
 EPS = 1e-6
+LONG_IMAGES = 6
+NEXT = 2
+COLUMNS = PIXELS // NEXT
 RUN = 8
 VECTOR_PIXELS = 304
 SCALAR_PIXELS = 168
-LAST_SHIFT = 40
+GPSIMD_PIXELS = PIXELS - VECTOR_PIXELS - SCALAR_PIXELS
+LAST_SHIFT = 72
 FIRST_IMAGES = 3
 FIRST_VECTOR_PIXELS = 312
 STORES_WAITING = 10
@@ -66,6 +70,31 @@ def tile_trgramkqv_pa_t_kernel(tc, token, Wk, Wv, out_0, out_1):
                 ],
             )
 
+        def regroup_long(b, pass_groups, vector_pixels):
+            target = grouped[b][:].rearrange("p g (e q) t -> p g q t e", e=NEXT)
+            source = raw[b][:].rearrange("p g t (q e) -> p g q t e", e=NEXT)
+            end = PIXELS if b < FIRST_IMAGES else PIXELS - 2 * GPSIMD_PIXELS
+            shares = []
+            for passes in pass_groups:
+                shares.append((nc.vector.tensor_copy, passes, 0, vector_pixels))
+                if b < FIRST_IMAGES:
+                    shares.append((nc.scalar.copy, passes, vector_pixels, PIXELS))
+                else:
+                    shares.append((nc.scalar.copy, slice(0, 1), vector_pixels, PIXELS))
+                    shares.append((nc.scalar.copy, slice(1, PASSES), vector_pixels, end))
+            for copy, passes, start, stop in shares:
+                columns = slice(start // NEXT, stop // NEXT)
+                copy(out=target[:, passes, columns], in_=source[:, passes, columns])
+            if end < PIXELS:
+                nc.gpsimd.tensor_scalar(
+                    out=target[:, 1, end // NEXT :].rearrange("p q t e -> p q e t"),
+                    in0=source[:, 1, end // NEXT :].rearrange("p q t e -> p q e t"),
+                    scalar1=1.0,
+                    scalar2=0.0,
+                    op0=ALU.mult,
+                    op1=ALU.add,
+                )
+
         def regroup(b, pass_groups):
             if b < FIRST_IMAGES:
                 vector_pixels, gpsimd_from = FIRST_VECTOR_PIXELS, PIXELS
@@ -74,6 +103,9 @@ def tile_trgramkqv_pa_t_kernel(tc, token, Wk, Wv, out_0, out_1):
                 gpsimd_from = VECTOR_PIXELS + SCALAR_PIXELS
             if b not in grouped:
                 grouped[b] = stage.tile([P, PASSES, PIXELS, PACK], BF16, align_bytes=64, name="grouped", bufs=2)
+            if b < LONG_IMAGES:
+                regroup_long(b, pass_groups, vector_pixels)
+                return
             for passes in pass_groups:
                 for copy, pixels in (
                     (nc.vector.tensor_copy, slice(0, vector_pixels)),
@@ -119,7 +151,8 @@ def tile_trgramkqv_pa_t_kernel(tc, token, Wk, Wv, out_0, out_1):
         def multiply_v(b, part=WHOLE):
             v_acc[b, part] = psum.tile([P, len(part), CHANNELS_OUT], F32, name="v_acc")
             for s in part:
-                pixels = slice(s * P, (s + 1) * P)
+                column = s % 2 * COLUMNS + s // 2 * P if b < LONG_IMAGES else s * P
+                pixels = slice(column, column + P)
                 for g in range(PASSES):
                     nc.tensor.matmul_mx(
                         out=v_acc[b, part][:, s - part.start, :],
@@ -133,7 +166,11 @@ def tile_trgramkqv_pa_t_kernel(tc, token, Wk, Wv, out_0, out_1):
 
         def square(b):
             squares[b] = norm.tile([P, PIXELS], F32, name="squares")
-            nc.scalar.activation(out=squares[b][:], in_=k_acc[b][:], func=ACT.Square)
+            out, k = squares[b][:], k_acc[b][:]
+            if b < LONG_IMAGES:
+                out = out.rearrange("p (q e) -> p q e", e=NEXT)
+                k = k.rearrange("p (e q) -> p q e", e=NEXT)
+            nc.scalar.activation(out=out, in_=k, func=ACT.Square)
 
         def pixels_of(part):
             return slice(part.start * P, part.stop * P)
@@ -148,6 +185,12 @@ def tile_trgramkqv_pa_t_kernel(tc, token, Wk, Wv, out_0, out_1):
         def store_v(b, part=WHOLE):
             vf = result.tile([P, len(part), CHANNELS_OUT], F32, name="vf")
             nc.scalar.copy(out=vf[:], in_=v_acc[b, part][:])
+            if b < LONG_IMAGES:
+                nc.sync.dma_start(
+                    out=out_1[b].rearrange("(h p e) c -> p h (e c)", p=P, e=NEXT),
+                    in_=vf[:].rearrange("p (h e) c -> p h (e c)", e=NEXT),
+                )
+                return
             nc.sync.dma_start(
                 out=out_1[b].rearrange("(s p) c -> p s c", p=P)[:, part.start : part.stop, :], in_=vf[:]
             )
@@ -158,11 +201,16 @@ def tile_trgramkqv_pa_t_kernel(tc, token, Wk, Wv, out_0, out_1):
 
         def store_k(b, part=WHOLE):
             kn = result.tile([P, len(part) * P], F32, name="kn")
+            out, factor, k = kn[:], inverse[b, part][:], k_acc[b][:, pixels_of(part)]
+            if b < LONG_IMAGES:
+                out = out.rearrange("p (q e) -> p q e", e=NEXT)
+                factor = factor.rearrange("p (q e) -> p q e", e=NEXT)
+                k = k.rearrange("p (e q) -> p q e", e=NEXT)
             nc.vector.scalar_tensor_tensor(
-                out=kn[:],
-                in0=inverse[b, part][:],
+                out=out,
+                in0=factor,
                 scalar=1.0 / EPS,
-                in1=k_acc[b][:, pixels_of(part)],
+                in1=k,
                 op0=ALU.min,
                 op1=ALU.mult,
             )

from contextlib import ExitStack

import concourse.mybir as mybir
from concourse.masks import make_identity

BF16 = mybir.dt.bfloat16
F32 = mybir.dt.float32
U32 = mybir.dt.uint32
U8 = mybir.dt.uint8
FP8X4 = mybir.dt.float8_e4m3fn_x4
ACT = mybir.ActivationFunctionType
ALU = mybir.AluOpType

P = 128
PACK = 4
K_PASS = P * PACK
IMAGES = 16
CHANNELS_IN = 1024
CHANNELS_OUT = 128
PIXELS = 512
PASSES = CHANNELS_IN // K_PASS
SLICES = PIXELS // P
EPS = 1e-6
LONG_IMAGES = 6
NEXT = 2
COLUMNS = PIXELS // NEXT
RUN = 8
VECTOR_PIXELS = 304
SCALAR_PIXELS = 168
GPSIMD_PIXELS = PIXELS - VECTOR_PIXELS - SCALAR_PIXELS
LAST_SHIFT = 72
FIRST_IMAGES = 3
FIRST_VECTOR_PIXELS = 312
STORES_WAITING = 10

WHOLE = range(SLICES)
HALVES = (range(0, SLICES // 2), range(SLICES // 2, SLICES))

FLOPS = 2 * 2 * IMAGES * CHANNELS_OUT * CHANNELS_IN * PIXELS


def tile_trgramkqv_pa_t_kernel(tc, token, Wk, Wv, out_0, out_1):
    nc = tc.nc
    with ExitStack() as ctx:
        const = ctx.enter_context(tc.tile_pool(name="const", bufs=1))
        raw_pool = ctx.enter_context(tc.tile_pool(name="raw", bufs=IMAGES))
        stage = ctx.enter_context(tc.tile_pool(name="stage", bufs=3))
        norm = ctx.enter_context(tc.tile_pool(name="norm", bufs=3))
        result = ctx.enter_context(tc.tile_pool(name="result", bufs=STORES_WAITING))
        psum = ctx.enter_context(tc.psum_pool(name="psum", bufs=2))
        ctx.enter_context(tc.manual_schedule())

        raw = {}
        grouped = {}
        codes = {}
        scales = {}
        k_acc = {}
        v_acc = {}
        squares = {}
        sums = {}
        inverse = {}

        def load(b, passes):
            if b not in raw:
                raw[b] = raw_pool.tile([P, PASSES, PACK, PIXELS], BF16, name="raw")
            nc.sync.dma_start(
                out=raw[b][:, passes].rearrange("p g t n -> p g (t n)"),
                in_=token[b].rearrange("(g p t) h w -> p g (t h w)", g=PASSES, p=P, t=PACK)[
                    :, passes
                ],
            )

        def regroup_long(b, pass_groups, vector_pixels):
            target = grouped[b][:].rearrange("p g (e q) t -> p g q t e", e=NEXT)
            source = raw[b][:].rearrange("p g t (q e) -> p g q t e", e=NEXT)
            end = PIXELS if b < FIRST_IMAGES else PIXELS - 2 * GPSIMD_PIXELS
            shares = []
            for passes in pass_groups:
                shares.append((nc.vector.tensor_copy, passes, 0, vector_pixels))
                if b < FIRST_IMAGES:
                    shares.append((nc.scalar.copy, passes, vector_pixels, PIXELS))
                else:
                    shares.append((nc.scalar.copy, slice(0, 1), vector_pixels, PIXELS))
                    shares.append((nc.scalar.copy, slice(1, PASSES), vector_pixels, end))
            for copy, passes, start, stop in shares:
                columns = slice(start // NEXT, stop // NEXT)
                copy(out=target[:, passes, columns], in_=source[:, passes, columns])
            if end < PIXELS:
                nc.gpsimd.tensor_scalar(
                    out=target[:, 1, end // NEXT :].rearrange("p q t e -> p q e t"),
                    in0=source[:, 1, end // NEXT :].rearrange("p q t e -> p q e t"),
                    scalar1=1.0,
                    scalar2=0.0,
                    op0=ALU.mult,
                    op1=ALU.add,
                )

        def regroup(b, pass_groups):
            if b < FIRST_IMAGES:
                vector_pixels, gpsimd_from = FIRST_VECTOR_PIXELS, PIXELS
            else:
                vector_pixels = VECTOR_PIXELS + (LAST_SHIFT if b == IMAGES - 1 else 0)
                gpsimd_from = VECTOR_PIXELS + SCALAR_PIXELS
            if b not in grouped:
                grouped[b] = stage.tile([P, PASSES, PIXELS, PACK], BF16, align_bytes=64, name="grouped", bufs=2)
            if b < LONG_IMAGES:
                regroup_long(b, pass_groups, vector_pixels)
                return
            for passes in pass_groups:
                for copy, pixels in (
                    (nc.vector.tensor_copy, slice(0, vector_pixels)),
                    (nc.scalar.copy, slice(vector_pixels, gpsimd_from)),
                ):
                    copy(
                        out=grouped[b][:, passes, pixels, :].rearrange("p g (c i) t -> p g c t i", i=RUN),
                        in_=raw[b][:, passes, :, pixels].rearrange("p g t (c i) -> p g c t i", i=RUN),
                    )
                if gpsimd_from < PIXELS:
                    pixels = slice(gpsimd_from, PIXELS)
                    nc.gpsimd.tensor_scalar(
                        out=grouped[b][:, passes, pixels, :],
                        in0=raw[b][:, passes, :, pixels].rearrange("p g t n -> p g n t"),
                        scalar1=1.0,
                        scalar2=0.0,
                        op0=ALU.mult,
                        op1=ALU.add,
                    )

        def quantise(b):
            codes[b] = stage.tile([P, PASSES, PIXELS], U32, align_bytes=64, name="codes")
            scales[b] = stage.tile([P, PASSES, PIXELS], U8, align_bytes=64, name="scales")
            nc.vector.quantize_mx(
                out=codes[b][:].rearrange("p g n -> p (g n)").bitcast(FP8X4),
                scales=scales[b][:].rearrange("p g n -> p (g n)"),
                in_=grouped[b][:].rearrange("p g n t -> p (g n t)"),
            )

        def multiply_k(b):
            k_acc[b] = psum.tile([P, PIXELS], F32, name="k_acc", bufs=4)
            for g in range(PASSES):
                nc.tensor.matmul_mx(
                    out=k_acc[b][:],
                    lhsT=w_codes[:, 0, g, :].bitcast(FP8X4),
                    lhsT_scale=w_scales[:, 0, g, :],
                    rhs=codes[b][:, g, :].bitcast(FP8X4),
                    rhs_scale=scales[b][:, g, :],
                    start=(g == 0),
                    stop=(g == PASSES - 1),
                )

        def multiply_v(b, part=WHOLE):
            v_acc[b, part] = psum.tile([P, len(part), CHANNELS_OUT], F32, name="v_acc")
            for s in part:
                column = s % 2 * COLUMNS + s // 2 * P if b < LONG_IMAGES else s * P
                pixels = slice(column, column + P)
                for g in range(PASSES):
                    nc.tensor.matmul_mx(
                        out=v_acc[b, part][:, s - part.start, :],
                        lhsT=codes[b][:, g, pixels].bitcast(FP8X4),
                        lhsT_scale=scales[b][:, g, pixels],
                        rhs=w_codes[:, 1, g, :].bitcast(FP8X4),
                        rhs_scale=w_scales[:, 1, g, :],
                        start=(g == 0),
                        stop=(g == PASSES - 1),
                    )

        def square(b):
            squares[b] = norm.tile([P, PIXELS], F32, name="squares")
            out, k = squares[b][:], k_acc[b][:]
            if b < LONG_IMAGES:
                out = out.rearrange("p (q e) -> p q e", e=NEXT)
                k = k.rearrange("p (e q) -> p q e", e=NEXT)
            nc.scalar.activation(out=out, in_=k, func=ACT.Square)

        def pixels_of(part):
            return slice(part.start * P, part.stop * P)

        def sum_squares(b, part=WHOLE):
            tag, bufs = ("k_acc", 4) if b == IMAGES - 1 else ("sums", 2)
            sums[b, part] = psum.tile([P, len(part) * P], F32, name="sums", tag=tag, bufs=bufs)
            nc.tensor.matmul(
                out=sums[b, part][:], lhsT=ones[:], rhs=squares[b][:, pixels_of(part)], start=True, stop=True
            )

        def store_v(b, part=WHOLE):
            vf = result.tile([P, len(part), CHANNELS_OUT], F32, name="vf")
            nc.scalar.copy(out=vf[:], in_=v_acc[b, part][:])
            if b < LONG_IMAGES:
                nc.sync.dma_start(
                    out=out_1[b].rearrange("(h p e) c -> p h (e c)", p=P, e=NEXT),
                    in_=vf[:].rearrange("p (h e) c -> p h (e c)", e=NEXT),
                )
                return
            nc.sync.dma_start(
                out=out_1[b].rearrange("(s p) c -> p s c", p=P)[:, part.start : part.stop, :], in_=vf[:]
            )

        def invert_norm(b, part=WHOLE):
            inverse[b, part] = norm.tile([P, len(part) * P], F32, name="inverse")
            nc.scalar.activation(out=inverse[b, part][:], in_=sums[b, part][:], func=ACT.Abs_reciprocal_sqrt)

        def store_k(b, part=WHOLE):
            kn = result.tile([P, len(part) * P], F32, name="kn")
            out, factor, k = kn[:], inverse[b, part][:], k_acc[b][:, pixels_of(part)]
            if b < LONG_IMAGES:
                out = out.rearrange("p (q e) -> p q e", e=NEXT)
                factor = factor.rearrange("p (q e) -> p q e", e=NEXT)
                k = k.rearrange("p (e q) -> p q e", e=NEXT)
            nc.vector.scalar_tensor_tensor(
                out=out,
                in0=factor,
                scalar=1.0 / EPS,
                in1=k,
                op0=ALU.min,
                op1=ALU.mult,
            )
            nc.sync.dma_start(out=out_0[b][:, pixels_of(part)], in_=kn[:])

        w_raw = const.tile([P, 2, CHANNELS_IN], BF16)
        load(0, slice(0, 1))
        load(0, slice(1, PASSES))
        nc.sync.dma_start(out=w_raw[:, 0, :], in_=Wk)
        nc.sync.dma_start(out=w_raw[:, 1, :], in_=Wv)
        load(1, slice(0, 1))
        load(1, slice(1, PASSES))
        for b in range(2, IMAGES):
            load(b, slice(0, PASSES))

        ident = const.tile([P, P], F32)
        make_identity(nc, ident[:])
        ones = const.tile([P, P], F32)
        nc.vector.memset(ones[:], 1.0)
        warm = const.tile([P, 1], F32)
        nc.scalar.activation(out=warm[:], in_=ones[:, 0:1], func=ACT.Abs_reciprocal_sqrt)

        regroup(0, (slice(0, 1), slice(1, PASSES)))
        quantise(0)

        w_words = w_raw[:].bitcast(F32).rearrange("c w (g p u) -> c w g u p", g=PASSES, p=P, u=2)
        w_grouped = const.tile([P, 2, PASSES * CHANNELS_OUT * PACK], BF16, align_bytes=64)
        w_codes = const.tile([P, 2, PASSES, CHANNELS_OUT], U32, align_bytes=64)
        w_scales = const.tile([P, 2, PASSES, CHANNELS_OUT], U8, align_bytes=64)
        for w in range(2):
            wt = psum.tile([P, PASSES, 2, CHANNELS_OUT], F32, name="wt", tag="sums")
            for g in range(PASSES):
                for u in range(2):
                    nc.tensor.transpose(wt[:, g, u, :], w_words[:, w, g, u, :], ident[:])
            nc.scalar.copy(
                out=w_grouped[:, w, :].bitcast(F32).rearrange("p (g c u) -> p g c u", g=PASSES, u=2),
                in_=wt[:].rearrange("p g u c -> p g c u"),
            )
            nc.vector.quantize_mx(
                out=w_codes[:, w].rearrange("p g c -> p (g c)").bitcast(FP8X4),
                scales=w_scales[:, w].rearrange("p g c -> p (g c)"),
                in_=w_grouped[:, w, :],
            )
        regroup(1, (slice(0, 1), slice(1, PASSES)))

        for b in range(IMAGES - 2):
            if 2 <= b:
                quantise(b)
            multiply_k(b)
            multiply_v(b)
            if 0 <= b - 2:
                store_k(b - 2)
            square(b)
            sum_squares(b)
            store_v(b)
            if b == 0:
                quantise(1)
            regroup(b + 2, (slice(0, PASSES),))
            invert_norm(b)

        last = IMAGES - 1
        quantise(last - 1)
        multiply_k(last - 1)
        multiply_v(last - 1)
        quantise(last)
        square(last - 1)
        multiply_k(last)
        for half in HALVES:
            sum_squares(last - 1, half)
        store_k(last - 3)
        store_v(last - 1)
        store_k(last - 2)
        square(last)
        for half in HALVES:
            invert_norm(last - 1, half)
        for half in HALVES:
            sum_squares(last, half)
        for half in HALVES:
            multiply_v(last, half)
        for half in HALVES:
            store_k(last - 1, half)
        for half in HALVES:
            invert_norm(last, half)
        for half in HALVES:
            store_k(last, half)
            store_v(last, half)
